import numpy as np
import ml_dtypes


def mxq(x, axis, fmt="e4m3"):
    dtype, down = {"e4m3": (ml_dtypes.float8_e4m3fn, 7), "e5m2": (ml_dtypes.float8_e5m2, 14)}[fmt]
    v = np.moveaxis(np.asarray(x, np.float32).astype(ml_dtypes.bfloat16).astype(np.float64), axis, -1)
    blocks = v.reshape(v.shape[:-1] + (-1, 32))
    amax = np.abs(blocks).max(-1, keepdims=True)
    byte = np.maximum(np.where(amax > 0, np.frexp(amax)[1] - 1 + 127, 0) - down, 1)
    scale = np.exp2(byte - 127.0)
    codes = (blocks / scale).astype(np.float32).astype(dtype).astype(np.float64)
    return np.moveaxis((codes * scale).reshape(v.shape), -1, axis)


WIDE = False


def mx_kscale(k):
    if not WIDE:
        return np.ones(k)
    levels = np.array([10, -10, 5, -5, 0])
    a = np.random.permutation(np.resize(levels, k // 512 * 4)).reshape(k // 512, 4)
    idx = np.arange(k)
    return np.exp2(a[idx // 512, idx % 128 // 32])


BF16 = ml_dtypes.bfloat16


def bf(x):
    return np.asarray(x, np.float32).astype(BF16)


def f64(x):
    return np.asarray(x).astype(np.float64)


B, D, H, W, K, M, F, NC = 2, 512, 128, 128, 128, 64, 128, 23
N = H * W
SD = np.sqrt(D)
AMP = 0.5
XV = 1.0 + AMP * AMP


def setup_inputs():
    r = mx_kscale(D)[:: D // K]
    r = r / r.max()
    m = r.min()
    img = np.random.standard_normal((B, D))[:, :, None, None]
    x = np.random.standard_normal((B, D, H, W)) + AMP * img
    c = np.random.standard_normal((K, D)) * 0.5
    sc = -(1.2 / SD) * (1.0 + 0.5 * np.random.standard_normal(K) / SD)
    c2 = (c * c).sum(1)
    g = (XV * D + c2) / (XV * D * m * m + c2 * r * r)
    return {"xb": bf(x * m), "codewords": bf(c * r[:, None]), "scale": bf(sc * g)}


def reference(xb, codewords, scale):
    X = f64(xb).reshape(B, D, N).transpose(0, 2, 1)
    C = f64(codewords)
    x2 = np.sum(X * X, axis=-1)
    c2 = np.sum(C * C, axis=-1)
    xc = mxq(X, 2, "e4m3") @ mxq(C, 1, "e4m3").T
    sl = f64(scale)[None, None, :] * (x2[:, :, None] + c2[None, None, :] - 2.0 * xc)
    e = np.exp(sl - sl.max(-1, keepdims=True))
    A = e / e.sum(-1, keepdims=True)
    agg = mxq(A, 1, "e4m3").transpose(0, 2, 1) @ mxq(X, 1, "e4m3")
    return agg - A.sum(1)[:, :, None] * C[None]

@@ -1,0 +1,203 @@
+from contextlib import ExitStack
+
+from concourse import mybir
+from concourse.masks import make_identity
+
+F32 = mybir.dt.float32
+BF16 = mybir.dt.bfloat16
+U32 = mybir.dt.uint32
+U8 = mybir.dt.uint8
+FP8X4 = mybir.dt.float8_e4m3fn_x4
+ALU = mybir.AluOpType
+ACT = mybir.ActivationFunctionType
+
+P = 128
+PACK = 4
+B, D, N, K = 2, 512, 128 * 128, 128
+GROUP = P * PACK
+LOAD = 4 * GROUP
+HALF = D // 2
+
+FLOPS = 2 * (2 * B * N * K * D)
+
+
+def quantise(nc, values, codes, scales):
+    nc.vector.quantize_mx(out=codes.bitcast(FP8X4), scales=scales, in_=values)
+
+
+def tile_depnet_pa_k_kernel(tc, xb, codewords, scale, out):
+    nc = tc.nc
+    with ExitStack() as stack:
+        consts = stack.enter_context(tc.tile_pool(name="consts", bufs=1))
+        loads = stack.enter_context(tc.tile_pool(name="loads", bufs=3))
+        work = stack.enter_context(tc.tile_pool(name="work", bufs=3))
+        small = stack.enter_context(tc.tile_pool(name="small", bufs=4))
+        ps_words = stack.enter_context(tc.psum_pool(name="ps_words", bufs=4))
+        ps_xc = stack.enter_context(tc.psum_pool(name="ps_xc", bufs=2))
+        ps_agg = stack.enter_context(tc.psum_pool(name="ps_agg", bufs=1))
+        ps_sum = stack.enter_context(tc.psum_pool(name="ps_sum", bufs=1))
+
+        ident = consts.tile([P, P], F32)
+        make_identity(nc, ident[:])
+
+        c_sb = consts.tile([K, D], BF16)
+        nc.sync.dma_start(out=c_sb[:], in_=codewords)
+        s_bf = consts.tile([P, K], BF16)
+        nc.scalar.dma_start(out=s_bf[:], in_=scale.partition_broadcast(P))
+
+        c_words = c_sb[:].bitcast(F32).rearrange("k (q v) -> k v q", v=2)
+        ct = ps_words.tile([P, 2, HALF], F32, tag="words")
+        for v in range(2):
+            nc.tensor.transpose(ct[:, v, 0:K], c_words[:, v, :], ident[:])
+        c_grouped = consts.tile([P, K * PACK], BF16, align_bytes=64)
+        nc.vector.tensor_copy(
+            out=c_grouped[:].bitcast(F32).rearrange("q (k v) -> q k v", v=2),
+            in_=ct[:, :, 0:K].rearrange("q v k -> q k v"),
+        )
+        c_codes = consts.tile([P, K], U32, align_bytes=64)
+        c_scales = consts.tile([P, K], U8, align_bytes=64)
+        quantise(nc, c_grouped[:], c_codes[:], c_scales[:])
+
+        c_squares = consts.tile([K, D], F32)
+        c2 = consts.tile([K, 1], F32)
+        nc.scalar.activation(out=c_squares[:], in_=c_sb[:], func=ACT.Square, accum_out=c2[:])
+        c2_rows = ps_words.tile([P, 2, HALF], F32, tag="words")
+        nc.tensor.transpose(c2_rows[:, 0, 0:K], c2[:, 0:1].to_broadcast([K, P]), ident[:])
+
+        two_s = consts.tile([P, K], F32)
+        nc.vector.tensor_scalar_mul(out=two_s[:], in0=s_bf[:], scalar1=2.0)
+        minus_s_c2 = consts.tile([P, K], F32)
+        nc.vector.scalar_tensor_tensor(
+            out=minus_s_c2[:], in0=s_bf[:], scalar=-1.0, in1=c2_rows[:, 0, 0:K],
+            op0=ALU.mult, op1=ALU.mult,
+        )
+
+        for b in range(B):
+            x_rows = xb[b].rearrange("(q j) h w -> q j (h w)", j=PACK)
+            agg = ps_agg.tile([K, D], F32)
+            a_sum = ps_sum.tile([K, 1], F32)
+
+            for c in range(N // LOAD):
+                x_sb = loads.tile([P, PACK * LOAD], BF16)
+                x_bf = x_sb[:].rearrange("q (j n) -> q j n", j=PACK)
+                nc.sync.dma_start(out=x_bf, in_=x_rows[:, :, c * LOAD : (c + 1) * LOAD])
+                x_words = x_sb[:].bitcast(F32).rearrange("q (j m v) -> q j m v", j=PACK, v=2)
+
+                for g in range(LOAD // GROUP):
+                    first = c == 0 and g == 0
+                    last = c == N // LOAD - 1 and g == LOAD // GROUP - 1
+
+                    xd_grouped = work.tile([P, GROUP * PACK], BF16, align_bytes=64)
+                    nc.vector.tensor_copy(
+                        out=xd_grouped[:].rearrange("q (t m j) -> q t m j", t=PACK, j=PACK),
+                        in_=x_bf[:, :, g * GROUP : (g + 1) * GROUP].rearrange(
+                            "q j (m t) -> q t m j", t=PACK
+                        ),
+                    )
+                    xd_codes = work.tile([P, GROUP], U32, align_bytes=64)
+                    xd_scales = work.tile([P, GROUP], U8, align_bytes=64)
+                    quantise(nc, xd_grouped[:], xd_codes[:], xd_scales[:])
+
+                    xn_grouped = work.tile([P, D * PACK], BF16, align_bytes=64)
+                    xn_words = xn_grouped[:].bitcast(F32).rearrange("m (d v) -> m d v", v=2)
+                    for half in range(2):
+                        xt = ps_words.tile([P, 2, HALF], F32, tag="words")
+                        for jj in range(2):
+                            for v in range(2):
+                                nc.tensor.transpose(
+                                    xt[:, v, jj * P : (jj + 1) * P],
+                                    x_words[:, 2 * half + jj, g * P : (g + 1) * P, v],
+                                    ident[:],
+                                )
+                        nc.scalar.copy(
+                            out=xn_words[:, half * HALF : (half + 1) * HALF, :],
+                            in_=xt[:].rearrange("m v d -> m d v"),
+                        )
+                    xn_codes = work.tile([P, D], U32, align_bytes=64)
+                    xn_scales = work.tile([P, D], U8, align_bytes=64)
+                    quantise(nc, xn_grouped[:], xn_codes[:], xn_scales[:])
+
+                    x2 = small.tile([P, PACK], F32)
+                    xn_by_quarter = xn_grouped[:].rearrange("m (d t) -> m t d", t=PACK)
+                    for t in range(PACK):
+                        squares = small.tile([P, D], BF16)
+                        nc.scalar.activation(
+                            out=squares[:], in_=xn_by_quarter[:, t, :], func=ACT.Square,
+                            accum_out=x2[:, t : t + 1],
+                        )
+                    half_x2 = small.tile([P, PACK], F32)
+                    nc.scalar.mul(out=half_x2[:], in_=x2[:], mul=0.5)
+
+                    xc = ps_xc.tile([P, PACK, K], F32)
+                    for t in range(PACK):
+                        nc.tensor.matmul_mx(
+                            out=xc[:, t, :],
+                            lhsT=xd_codes[:, t * P : (t + 1) * P].bitcast(FP8X4),
+                            lhsT_scale=xd_scales[:, t * P : (t + 1) * P],
+                            rhs=c_codes[:].bitcast(FP8X4),
+                            rhs_scale=c_scales[:],
+                            start=True,
+                            stop=True,
+                        )
+                    neg_sl = work.tile([P, PACK, K], F32)
+                    for t in range(PACK):
+                        nc.vector.scalar_tensor_tensor(
+                            out=neg_sl[:, t, :], in0=xc[:, t, :], scalar=half_x2[:, t : t + 1],
+                            in1=two_s[:], op0=ALU.subtract, op1=ALU.mult,
+                        )
+                    nc.vector.tensor_tensor(
+                        out=neg_sl[:], in0=neg_sl[:],
+                        in1=minus_s_c2[:].unsqueeze(1).to_broadcast([P, PACK, K]), op=ALU.add,
+                    )
+
+                    lowest = small.tile([P, PACK], F32)
+                    nc.vector.tensor_reduce(
+                        out=lowest[:], in_=neg_sl[:], axis=mybir.AxisListType.X, op=ALU.min
+                    )
+                    e = work.tile([P, PACK, K], F32)
+                    e_sum = small.tile([P, PACK], F32)
+                    for t in range(PACK):
+                        nc.scalar.activation(
+                            out=e[:, t, :], in_=neg_sl[:, t, :], func=ACT.Exp,
+                            bias=lowest[:, t : t + 1], scale=-1.0, accum_out=e_sum[:, t : t + 1],
+                        )
+                    inv_sum = small.tile([P, PACK], F32)
+                    nc.vector.reciprocal(out=inv_sum[:], in_=e_sum[:])
+
+                    a_grouped = work.tile([P, K * PACK], BF16, align_bytes=64)
+                    nc.vector.tensor_tensor(
+                        out=a_grouped[:].rearrange("m (k t) -> m k t", t=PACK),
+                        in0=e[:].rearrange("m t k -> m k t"),
+                        in1=inv_sum[:].unsqueeze(1).to_broadcast([P, K, PACK]),
+                        op=ALU.mult,
+                    )
+                    a_codes = work.tile([P, K], U32, align_bytes=64)
+                    a_scales = work.tile([P, K], U8, align_bytes=64)
+                    quantise(nc, a_grouped[:], a_codes[:], a_scales[:])
+
+                    nc.tensor.matmul_mx(
+                        out=agg[:],
+                        lhsT=a_codes[:].bitcast(FP8X4),
+                        lhsT_scale=a_scales[:],
+                        rhs=xn_codes[:].bitcast(FP8X4),
+                        rhs_scale=xn_scales[:],
+                        start=first,
+                        stop=last,
+                    )
+                    for t in range(PACK):
+                        nc.tensor.matmul(
+                            out=a_sum[:], lhsT=e[:, t, :], rhs=inv_sum[:, t : t + 1],
+                            start=first and t == 0, stop=last and t == PACK - 1,
+                        )
+
+            minus_a_sum = small.tile([K, 1], F32)
+            nc.vector.tensor_scalar_mul(out=minus_a_sum[:], in0=a_sum[:], scalar1=-1.0)
+            result = work.tile([K, D], F32)
+            nc.vector.scalar_tensor_tensor(
+                out=result[:].rearrange("k (q j) -> k q j", j=PACK),
+                in0=c_sb[:].rearrange("k (q j) -> k q j", j=PACK),
+                scalar=minus_a_sum[:, 0:1],
+                in1=agg[:].rearrange("k (j q) -> k q j", j=PACK),
+                op0=ALU.mult, op1=ALU.add,
+            )
+            nc.sync.dma_start(out=out[b], in_=result[:])

@@ -17,6 +17,13 @@ B, D, N, K = 2, 512, 128 * 128, 128
 GROUP = P * PACK
 LOAD = 4 * GROUP
 HALF = D // 2
+GROUPS_PER_LOAD = LOAD // GROUP
+GROUPS_PER_IMAGE = N // GROUP
+GROUPS = B * GROUPS_PER_IMAGE
+LOADS_PER_IMAGE = N // LOAD
+LOADS = B * LOADS_PER_IMAGE
+LOADS_AHEAD = 2
+DEPTH = 7
 
 FLOPS = 2 * (2 * B * N * K * D)
 
@@ -29,9 +36,8 @@ def tile_depnet_pa_k_kernel(tc, xb, codewords, scale, out):
     nc = tc.nc
     with ExitStack() as stack:
         consts = stack.enter_context(tc.tile_pool(name="consts", bufs=1))
-        loads = stack.enter_context(tc.tile_pool(name="loads", bufs=3))
-        work = stack.enter_context(tc.tile_pool(name="work", bufs=3))
-        small = stack.enter_context(tc.tile_pool(name="small", bufs=4))
+        loads = stack.enter_context(tc.tile_pool(name="loads", bufs=LOADS_AHEAD + 1))
+        work = stack.enter_context(tc.tile_pool(name="work", bufs=DEPTH))
         ps_words = stack.enter_context(tc.psum_pool(name="ps_words", bufs=4))
         ps_xc = stack.enter_context(tc.psum_pool(name="ps_xc", bufs=2))
         ps_agg = stack.enter_context(tc.psum_pool(name="ps_agg", bufs=1))
@@ -72,132 +78,220 @@ def tile_depnet_pa_k_kernel(tc, xb, codewords, scale, out):
             op0=ALU.mult, op1=ALU.mult,
         )
 
-        for b in range(B):
-            x_rows = xb[b].rearrange("(q j) h w -> q j (h w)", j=PACK)
-            agg = ps_agg.tile([K, D], F32)
-            a_sum = ps_sum.tile([K, 1], F32)
+        kept = {}
 
-            for c in range(N // LOAD):
-                x_sb = loads.tile([P, PACK * LOAD], BF16)
-                x_bf = x_sb[:].rearrange("q (j n) -> q j n", j=PACK)
-                nc.sync.dma_start(out=x_bf, in_=x_rows[:, :, c * LOAD : (c + 1) * LOAD])
-                x_words = x_sb[:].bitcast(F32).rearrange("q (j m v) -> q j m v", j=PACK, v=2)
+        def load(c):
+            x_rows = xb[c // LOADS_PER_IMAGE].rearrange("(q j) h w -> q j (h w)", j=PACK)
+            first_n = (c % LOADS_PER_IMAGE) * LOAD
+            x_sb = loads.tile([P, PACK * LOAD], BF16)
+            nc.sync.dma_start(
+                out=x_sb[:].rearrange("q (j n) -> q j n", j=PACK),
+                in_=x_rows[:, :, first_n : first_n + LOAD],
+            )
+            kept["x", c] = x_sb
 
-                for g in range(LOAD // GROUP):
-                    first = c == 0 and g == 0
-                    last = c == N // LOAD - 1 and g == LOAD // GROUP - 1
+        def regroup_channels(g):
+            x_bf = kept["x", g // GROUPS_PER_LOAD][:].rearrange("q (j n) -> q j n", j=PACK)
+            first_n = (g % GROUPS_PER_LOAD) * GROUP
+            xd_grouped = work.tile([P, GROUP * PACK], BF16, align_bytes=64)
+            nc.vector.tensor_copy(
+                out=xd_grouped[:].rearrange("q (t m j) -> q t m j", t=PACK, j=PACK),
+                in_=x_bf[:, :, first_n : first_n + GROUP].rearrange("q j (m t) -> q t m j", t=PACK),
+            )
+            kept["xd_grouped", g] = xd_grouped
 
-                    xd_grouped = work.tile([P, GROUP * PACK], BF16, align_bytes=64)
-                    nc.vector.tensor_copy(
-                        out=xd_grouped[:].rearrange("q (t m j) -> q t m j", t=PACK, j=PACK),
-                        in_=x_bf[:, :, g * GROUP : (g + 1) * GROUP].rearrange(
-                            "q j (m t) -> q t m j", t=PACK
-                        ),
-                    )
-                    xd_codes = work.tile([P, GROUP], U32, align_bytes=64)
-                    xd_scales = work.tile([P, GROUP], U8, align_bytes=64)
-                    quantise(nc, xd_grouped[:], xd_codes[:], xd_scales[:])
+        def quantise_along_channels(g):
+            xd_codes = work.tile([P, GROUP], U32, align_bytes=64)
+            xd_scales = work.tile([P, GROUP], U8, align_bytes=64)
+            quantise(nc, kept["xd_grouped", g][:], xd_codes[:], xd_scales[:])
+            kept["xd_codes", g] = xd_codes
+            kept["xd_scales", g] = xd_scales
 
-                    xn_grouped = work.tile([P, D * PACK], BF16, align_bytes=64)
-                    xn_words = xn_grouped[:].bitcast(F32).rearrange("m (d v) -> m d v", v=2)
-                    for half in range(2):
-                        xt = ps_words.tile([P, 2, HALF], F32, tag="words")
-                        for jj in range(2):
-                            for v in range(2):
-                                nc.tensor.transpose(
-                                    xt[:, v, jj * P : (jj + 1) * P],
-                                    x_words[:, 2 * half + jj, g * P : (g + 1) * P, v],
-                                    ident[:],
-                                )
-                        nc.scalar.copy(
-                            out=xn_words[:, half * HALF : (half + 1) * HALF, :],
-                            in_=xt[:].rearrange("m v d -> m d v"),
+        def transpose_words(g):
+            x_words = (
+                kept["x", g // GROUPS_PER_LOAD][:]
+                .bitcast(F32)
+                .rearrange("q (j m v) -> q j m v", j=PACK, v=2)
+            )
+            first_m = (g % GROUPS_PER_LOAD) * P
+            for half in range(2):
+                xt = ps_words.tile([P, 2, HALF], F32, tag="words")
+                for jj in range(2):
+                    for v in range(2):
+                        nc.tensor.transpose(
+                            xt[:, v, jj * P : (jj + 1) * P],
+                            x_words[:, 2 * half + jj, first_m : first_m + P, v],
+                            ident[:],
                         )
-                    xn_codes = work.tile([P, D], U32, align_bytes=64)
-                    xn_scales = work.tile([P, D], U8, align_bytes=64)
-                    quantise(nc, xn_grouped[:], xn_codes[:], xn_scales[:])
+                kept["xt", g, half] = xt
 
-                    x2 = small.tile([P, PACK], F32)
-                    xn_by_quarter = xn_grouped[:].rearrange("m (d t) -> m t d", t=PACK)
-                    for t in range(PACK):
-                        squares = small.tile([P, D], BF16)
-                        nc.scalar.activation(
-                            out=squares[:], in_=xn_by_quarter[:, t, :], func=ACT.Square,
-                            accum_out=x2[:, t : t + 1],
-                        )
-                    half_x2 = small.tile([P, PACK], F32)
-                    nc.scalar.mul(out=half_x2[:], in_=x2[:], mul=0.5)
+        def copy_words_out(g):
+            xn_grouped = work.tile([P, D * PACK], BF16, align_bytes=64)
+            xn_words = xn_grouped[:].bitcast(F32).rearrange("m (d v) -> m d v", v=2)
+            for half in range(2):
+                nc.scalar.copy(
+                    out=xn_words[:, half * HALF : (half + 1) * HALF, :],
+                    in_=kept["xt", g, half][:].rearrange("m v d -> m d v"),
+                )
+            kept["xn_grouped", g] = xn_grouped
 
-                    xc = ps_xc.tile([P, PACK, K], F32)
-                    for t in range(PACK):
-                        nc.tensor.matmul_mx(
-                            out=xc[:, t, :],
-                            lhsT=xd_codes[:, t * P : (t + 1) * P].bitcast(FP8X4),
-                            lhsT_scale=xd_scales[:, t * P : (t + 1) * P],
-                            rhs=c_codes[:].bitcast(FP8X4),
-                            rhs_scale=c_scales[:],
-                            start=True,
-                            stop=True,
-                        )
-                    neg_sl = work.tile([P, PACK, K], F32)
-                    for t in range(PACK):
-                        nc.vector.scalar_tensor_tensor(
-                            out=neg_sl[:, t, :], in0=xc[:, t, :], scalar=half_x2[:, t : t + 1],
-                            in1=two_s[:], op0=ALU.subtract, op1=ALU.mult,
-                        )
-                    nc.vector.tensor_tensor(
-                        out=neg_sl[:], in0=neg_sl[:],
-                        in1=minus_s_c2[:].unsqueeze(1).to_broadcast([P, PACK, K]), op=ALU.add,
-                    )
+        def quantise_along_positions(g):
+            xn_codes = work.tile([P, D], U32, align_bytes=64)
+            xn_scales = work.tile([P, D], U8, align_bytes=64)
+            quantise(nc, kept["xn_grouped", g][:], xn_codes[:], xn_scales[:])
+            kept["xn_codes", g] = xn_codes
+            kept["xn_scales", g] = xn_scales
 
-                    lowest = small.tile([P, PACK], F32)
-                    nc.vector.tensor_reduce(
-                        out=lowest[:], in_=neg_sl[:], axis=mybir.AxisListType.X, op=ALU.min
-                    )
-                    e = work.tile([P, PACK, K], F32)
-                    e_sum = small.tile([P, PACK], F32)
-                    for t in range(PACK):
-                        nc.scalar.activation(
-                            out=e[:, t, :], in_=neg_sl[:, t, :], func=ACT.Exp,
-                            bias=lowest[:, t : t + 1], scale=-1.0, accum_out=e_sum[:, t : t + 1],
-                        )
-                    inv_sum = small.tile([P, PACK], F32)
-                    nc.vector.reciprocal(out=inv_sum[:], in_=e_sum[:])
+        def square_norms(g):
+            x2 = work.tile([P, PACK], F32)
+            xn_by_quarter = kept["xn_grouped", g][:].rearrange("m (d t) -> m t d", t=PACK)
+            for t in range(PACK):
+                squares = work.tile([P, D], BF16)
+                nc.scalar.activation(
+                    out=squares[:], in_=xn_by_quarter[:, t, :], func=ACT.Square,
+                    accum_out=x2[:, t : t + 1],
+                )
+            half_x2 = work.tile([P, PACK], F32)
+            nc.scalar.mul(out=half_x2[:], in_=x2[:], mul=0.5)
+            kept["half_x2", g] = half_x2
 
-                    a_grouped = work.tile([P, K * PACK], BF16, align_bytes=64)
-                    nc.vector.tensor_tensor(
-                        out=a_grouped[:].rearrange("m (k t) -> m k t", t=PACK),
-                        in0=e[:].rearrange("m t k -> m k t"),
-                        in1=inv_sum[:].unsqueeze(1).to_broadcast([P, K, PACK]),
-                        op=ALU.mult,
-                    )
-                    a_codes = work.tile([P, K], U32, align_bytes=64)
-                    a_scales = work.tile([P, K], U8, align_bytes=64)
-                    quantise(nc, a_grouped[:], a_codes[:], a_scales[:])
+        def first_product(g):
+            xc = ps_xc.tile([P, PACK, K], F32)
+            for t in range(PACK):
+                nc.tensor.matmul_mx(
+                    out=xc[:, t, :],
+                    lhsT=kept["xd_codes", g][:, t * P : (t + 1) * P].bitcast(FP8X4),
+                    lhsT_scale=kept["xd_scales", g][:, t * P : (t + 1) * P],
+                    rhs=c_codes[:].bitcast(FP8X4),
+                    rhs_scale=c_scales[:],
+                    start=True,
+                    stop=True,
+                )
+            kept["xc", g] = xc
 
-                    nc.tensor.matmul_mx(
-                        out=agg[:],
-                        lhsT=a_codes[:].bitcast(FP8X4),
-                        lhsT_scale=a_scales[:],
-                        rhs=xn_codes[:].bitcast(FP8X4),
-                        rhs_scale=xn_scales[:],
-                        start=first,
-                        stop=last,
-                    )
-                    for t in range(PACK):
-                        nc.tensor.matmul(
-                            out=a_sum[:], lhsT=e[:, t, :], rhs=inv_sum[:, t : t + 1],
-                            start=first and t == 0, stop=last and t == PACK - 1,
-                        )
+        def scale_distances(g):
+            neg_sl = work.tile([P, PACK, K], F32)
+            for t in range(PACK):
+                nc.vector.scalar_tensor_tensor(
+                    out=neg_sl[:, t, :], in0=kept["xc", g][:, t, :],
+                    scalar=kept["half_x2", g][:, t : t + 1], in1=two_s[:],
+                    op0=ALU.subtract, op1=ALU.mult,
+                )
+            kept["neg_sl", g] = neg_sl
 
-            minus_a_sum = small.tile([K, 1], F32)
-            nc.vector.tensor_scalar_mul(out=minus_a_sum[:], in0=a_sum[:], scalar1=-1.0)
+        def add_codeword_term(g):
+            neg_sl = kept["neg_sl", g]
+            nc.vector.tensor_tensor(
+                out=neg_sl[:], in0=neg_sl[:],
+                in1=minus_s_c2[:].unsqueeze(1).to_broadcast([P, PACK, K]), op=ALU.add,
+            )
+
+        def lowest_negated_logit(g):
+            lowest = work.tile([P, PACK], F32)
+            nc.vector.tensor_reduce(
+                out=lowest[:], in_=kept["neg_sl", g][:], axis=mybir.AxisListType.X, op=ALU.min
+            )
+            kept["lowest", g] = lowest
+
+        def exponentials(g):
+            e = work.tile([P, PACK, K], F32)
+            e_sum = work.tile([P, PACK], F32)
+            for t in range(PACK):
+                nc.scalar.activation(
+                    out=e[:, t, :], in_=kept["neg_sl", g][:, t, :], func=ACT.Exp,
+                    bias=kept["lowest", g][:, t : t + 1], scale=-1.0,
+                    accum_out=e_sum[:, t : t + 1],
+                )
+            kept["e", g] = e
+            kept["e_sum", g] = e_sum
+
+        def invert_sums(g):
+            inv_sum = work.tile([P, PACK], F32)
+            nc.vector.reciprocal(out=inv_sum[:], in_=kept["e_sum", g][:])
+            kept["inv_sum", g] = inv_sum
+
+        def normalise(g):
+            a_grouped = work.tile([P, K * PACK], BF16, align_bytes=64)
+            nc.vector.tensor_tensor(
+                out=a_grouped[:].rearrange("m (k t) -> m k t", t=PACK),
+                in0=kept["e", g][:].rearrange("m t k -> m k t"),
+                in1=kept["inv_sum", g][:].unsqueeze(1).to_broadcast([P, K, PACK]),
+                op=ALU.mult,
+            )
+            kept["a_grouped", g] = a_grouped
+
+        def quantise_weights(g):
+            a_codes = work.tile([P, K], U32, align_bytes=64)
+            a_scales = work.tile([P, K], U8, align_bytes=64)
+            quantise(nc, kept["a_grouped", g][:], a_codes[:], a_scales[:])
+            kept["a_codes", g] = a_codes
+            kept["a_scales", g] = a_scales
+
+        def second_product(g):
+            b = g // GROUPS_PER_IMAGE
+            first = g % GROUPS_PER_IMAGE == 0
+            last = g % GROUPS_PER_IMAGE == GROUPS_PER_IMAGE - 1
+            if first:
+                agg = ps_agg.tile([K, D], F32)
+                a_sum = ps_sum.tile([K, 1], F32)
+                kept["agg", b] = agg
+                kept["a_sum", b] = a_sum
+            nc.tensor.matmul_mx(
+                out=kept["agg", b][:],
+                lhsT=kept["a_codes", g][:].bitcast(FP8X4),
+                lhsT_scale=kept["a_scales", g][:],
+                rhs=kept["xn_codes", g][:].bitcast(FP8X4),
+                rhs_scale=kept["xn_scales", g][:],
+                start=first,
+                stop=last,
+            )
+            for t in range(PACK):
+                nc.tensor.matmul(
+                    out=kept["a_sum", b][:], lhsT=kept["e", g][:, t, :],
+                    rhs=kept["inv_sum", g][:, t : t + 1],
+                    start=first and t == 0, stop=last and t == PACK - 1,
+                )
+
+        def finish_image(b):
+            minus_a_sum = work.tile([K, 1], F32)
+            nc.vector.tensor_scalar_mul(out=minus_a_sum[:], in0=kept["a_sum", b][:], scalar1=-1.0)
             result = work.tile([K, D], F32)
             nc.vector.scalar_tensor_tensor(
                 out=result[:].rearrange("k (q j) -> k q j", j=PACK),
                 in0=c_sb[:].rearrange("k (q j) -> k q j", j=PACK),
                 scalar=minus_a_sum[:, 0:1],
-                in1=agg[:].rearrange("k (j q) -> k q j", j=PACK),
+                in1=kept["agg", b][:].rearrange("k (j q) -> k q j", j=PACK),
                 op0=ALU.mult, op1=ALU.add,
             )
             nc.sync.dma_start(out=out[b], in_=result[:])
+
+        def run(stage, g):
+            if 0 <= g < GROUPS:
+                stage(g)
+
+        with tc.manual_schedule():
+            for c in range(LOADS_AHEAD):
+                load(c)
+            for i in range(GROUPS + DEPTH):
+                if i % GROUPS_PER_LOAD == 0 and i // GROUPS_PER_LOAD + LOADS_AHEAD < LOADS:
+                    load(i // GROUPS_PER_LOAD + LOADS_AHEAD)
+
+                run(first_product, i - 1)
+                run(second_product, i - 5)
+                run(transpose_words, i)
+
+                run(copy_words_out, i - 1)
+                run(exponentials, i - 3)
+                run(square_norms, i - 1)
+
+                if i >= 6 and (i - 6) % GROUPS_PER_IMAGE == GROUPS_PER_IMAGE - 1:
+                    finish_image((i - 6) // GROUPS_PER_IMAGE)
+                run(invert_sums, i - 4)
+                run(regroup_channels, i)
+                run(scale_distances, i - 2)
+                run(normalise, i - 4)
+                run(add_codeword_term, i - 2)
+                run(quantise_along_channels, i)
+                run(lowest_negated_logit, i - 2)
+                run(quantise_weights, i - 4)
+                run(quantise_along_positions, i - 2)

@@ -23,7 +23,9 @@ GROUPS = B * GROUPS_PER_IMAGE
 LOADS_PER_IMAGE = N // LOAD
 LOADS = B * LOADS_PER_IMAGE
 LOADS_AHEAD = 2
-DEPTH = 7
+LAST_LAG = 8
+NEAR = 4
+FAR = 7
 
 FLOPS = 2 * (2 * B * N * K * D)
 
@@ -37,9 +39,11 @@ def tile_depnet_pa_k_kernel(tc, xb, codewords, scale, out):
     with ExitStack() as stack:
         consts = stack.enter_context(tc.tile_pool(name="consts", bufs=1))
         loads = stack.enter_context(tc.tile_pool(name="loads", bufs=LOADS_AHEAD + 1))
-        work = stack.enter_context(tc.tile_pool(name="work", bufs=DEPTH))
+        near = stack.enter_context(tc.tile_pool(name="near", bufs=NEAR))
+        far = stack.enter_context(tc.tile_pool(name="far", bufs=FAR))
         ps_words = stack.enter_context(tc.psum_pool(name="ps_words", bufs=4))
-        ps_xc = stack.enter_context(tc.psum_pool(name="ps_xc", bufs=2))
+        ps_xc = stack.enter_context(tc.psum_pool(name="ps_xc", bufs=1))
+        ps_y = stack.enter_context(tc.psum_pool(name="ps_y", bufs=1))
         ps_agg = stack.enter_context(tc.psum_pool(name="ps_agg", bufs=1))
         ps_sum = stack.enter_context(tc.psum_pool(name="ps_sum", bufs=1))
 
@@ -67,15 +71,16 @@ def tile_depnet_pa_k_kernel(tc, xb, codewords, scale, out):
         c_squares = consts.tile([K, D], F32)
         c2 = consts.tile([K, 1], F32)
         nc.scalar.activation(out=c_squares[:], in_=c_sb[:], func=ACT.Square, accum_out=c2[:])
-        c2_rows = ps_words.tile([P, 2, HALF], F32, tag="words")
-        nc.tensor.transpose(c2_rows[:, 0, 0:K], c2[:, 0:1].to_broadcast([K, P]), ident[:])
 
-        two_s = consts.tile([P, K], F32)
-        nc.vector.tensor_scalar_mul(out=two_s[:], in0=s_bf[:], scalar1=2.0)
-        minus_s_c2 = consts.tile([P, K], F32)
-        nc.vector.scalar_tensor_tensor(
-            out=minus_s_c2[:], in0=s_bf[:], scalar=-1.0, in1=c2_rows[:, 0, 0:K],
-            op0=ALU.mult, op1=ALU.mult,
+        minus_s = consts.tile([P, K], F32)
+        nc.vector.tensor_scalar_mul(out=minus_s[:], in0=s_bf[:], scalar1=-1.0)
+        minus_s_cols = ps_words.tile([P, 2, HALF], F32, tag="words")
+        nc.tensor.transpose(minus_s_cols[:, 0, 0:P], minus_s[:], ident[:])
+        two_s = consts.tile([K, 1], F32)
+        nc.vector.tensor_scalar_mul(out=two_s[:], in0=minus_s_cols[:, 0, 0:1], scalar1=-2.0)
+        minus_s_c2 = consts.tile([K, 1], F32)
+        nc.vector.tensor_tensor(
+            out=minus_s_c2[:], in0=minus_s_cols[:, 0, 0:1], in1=c2[:], op=ALU.mult
         )
 
         kept = {}
@@ -93,16 +98,16 @@ def tile_depnet_pa_k_kernel(tc, xb, codewords, scale, out):
         def regroup_channels(g):
             x_bf = kept["x", g // GROUPS_PER_LOAD][:].rearrange("q (j n) -> q j n", j=PACK)
             first_n = (g % GROUPS_PER_LOAD) * GROUP
-            xd_grouped = work.tile([P, GROUP * PACK], BF16, align_bytes=64)
+            xd_grouped = near.tile([P, GROUP * PACK], BF16, align_bytes=64)
             nc.vector.tensor_copy(
-                out=xd_grouped[:].rearrange("q (t m j) -> q t m j", t=PACK, j=PACK),
-                in_=x_bf[:, :, first_n : first_n + GROUP].rearrange("q j (m t) -> q t m j", t=PACK),
+                out=xd_grouped[:].rearrange("q (c i j) -> q c j i", i=4, j=PACK),
+                in_=x_bf[:, :, first_n : first_n + GROUP].rearrange("q j (c i) -> q c j i", i=4),
             )
             kept["xd_grouped", g] = xd_grouped
 
         def quantise_along_channels(g):
-            xd_codes = work.tile([P, GROUP], U32, align_bytes=64)
-            xd_scales = work.tile([P, GROUP], U8, align_bytes=64)
+            xd_codes = near.tile([P, GROUP], U32, align_bytes=64)
+            xd_scales = near.tile([P, GROUP], U8, align_bytes=64)
             quantise(nc, kept["xd_grouped", g][:], xd_codes[:], xd_scales[:])
             kept["xd_codes", g] = xd_codes
             kept["xd_scales", g] = xd_scales
@@ -125,77 +130,86 @@ def tile_depnet_pa_k_kernel(tc, xb, codewords, scale, out):
                         )
                 kept["xt", g, half] = xt
 
-        def copy_words_out(g):
-            xn_grouped = work.tile([P, D * PACK], BF16, align_bytes=64)
-            xn_words = xn_grouped[:].bitcast(F32).rearrange("m (d v) -> m d v", v=2)
-            for half in range(2):
-                nc.scalar.copy(
-                    out=xn_words[:, half * HALF : (half + 1) * HALF, :],
-                    in_=kept["xt", g, half][:].rearrange("m v d -> m d v"),
-                )
-            kept["xn_grouped", g] = xn_grouped
+        def copy_words_out(g, half, copy):
+            if half == 0:
+                xn_grouped = near.tile([P, D * PACK], BF16, align_bytes=64)
+                kept["xn_grouped", g] = xn_grouped
+            xn_words = kept["xn_grouped", g][:].bitcast(F32).rearrange("m (d v) -> m d v", v=2)
+            copy(
+                out=xn_words[:, half * HALF : (half + 1) * HALF, :],
+                in_=kept["xt", g, half][:].rearrange("m v d -> m d v"),
+            )
+
+        def copy_first_half_out(g):
+            copy_words_out(g, 0, nc.scalar.copy)
+
+        def copy_second_half_out(g):
+            copy_words_out(g, 1, nc.vector.tensor_copy)
 
         def quantise_along_positions(g):
-            xn_codes = work.tile([P, D], U32, align_bytes=64)
-            xn_scales = work.tile([P, D], U8, align_bytes=64)
+            xn_codes = far.tile([P, D], U32, align_bytes=64)
+            xn_scales = far.tile([P, D], U8, align_bytes=64)
             quantise(nc, kept["xn_grouped", g][:], xn_codes[:], xn_scales[:])
             kept["xn_codes", g] = xn_codes
             kept["xn_scales", g] = xn_scales
 
         def square_norms(g):
-            x2 = work.tile([P, PACK], F32)
+            x2 = far.tile([P, PACK], F32)
             xn_by_quarter = kept["xn_grouped", g][:].rearrange("m (d t) -> m t d", t=PACK)
             for t in range(PACK):
-                squares = work.tile([P, D], BF16)
+                squares = far.tile([P, D], BF16)
                 nc.scalar.activation(
                     out=squares[:], in_=xn_by_quarter[:, t, :], func=ACT.Square,
                     accum_out=x2[:, t : t + 1],
                 )
-            half_x2 = work.tile([P, PACK], F32)
-            nc.scalar.mul(out=half_x2[:], in_=x2[:], mul=0.5)
-            kept["half_x2", g] = half_x2
+            kept["x2", g] = x2
 
         def first_product(g):
-            xc = ps_xc.tile([P, PACK, K], F32)
-            for t in range(PACK):
-                nc.tensor.matmul_mx(
-                    out=xc[:, t, :],
-                    lhsT=kept["xd_codes", g][:, t * P : (t + 1) * P].bitcast(FP8X4),
-                    lhsT_scale=kept["xd_scales", g][:, t * P : (t + 1) * P],
-                    rhs=c_codes[:].bitcast(FP8X4),
-                    rhs_scale=c_scales[:],
-                    start=True,
-                    stop=True,
-                )
+            xc = ps_xc.tile([K, GROUP], F32)
+            nc.tensor.matmul_mx(
+                out=xc[:],
+                lhsT=c_codes[:].bitcast(FP8X4),
+                lhsT_scale=c_scales[:],
+                rhs=kept["xd_codes", g][:].bitcast(FP8X4),
+                rhs_scale=kept["xd_scales", g][:],
+                start=True,
+                stop=True,
+            )
             kept["xc", g] = xc
 
-        def scale_distances(g):
-            neg_sl = work.tile([P, PACK, K], F32)
+        def codeword_factors(g):
+            y = near.tile([K, PACK, P], F32)
+            nc.scalar.activation(
+                out=y[:], in_=kept["xc", g][:].rearrange("k (m t) -> k t m", t=PACK),
+                func=ACT.Identity, scale=two_s[:, 0:1], bias=minus_s_c2[:, 0:1],
+            )
+            kept["y", g] = y
+
+        def transpose_logits(g):
+            y_rows = ps_y.tile([P, PACK, K], F32)
+            for t in range(PACK):
+                nc.tensor.transpose(y_rows[:, t, :], kept["y", g][:, t, :], ident[:])
+            kept["y_rows", g] = y_rows
+
+        def add_position_term(g):
+            neg_sl = near.tile([P, PACK, K], F32)
             for t in range(PACK):
                 nc.vector.scalar_tensor_tensor(
-                    out=neg_sl[:, t, :], in0=kept["xc", g][:, t, :],
-                    scalar=kept["half_x2", g][:, t : t + 1], in1=two_s[:],
-                    op0=ALU.subtract, op1=ALU.mult,
+                    out=neg_sl[:, t, :], in0=minus_s[:], scalar=kept["x2", g][:, t : t + 1],
+                    in1=kept["y_rows", g][:, t, :], op0=ALU.mult, op1=ALU.add,
                 )
             kept["neg_sl", g] = neg_sl
 
-        def add_codeword_term(g):
-            neg_sl = kept["neg_sl", g]
-            nc.vector.tensor_tensor(
-                out=neg_sl[:], in0=neg_sl[:],
-                in1=minus_s_c2[:].unsqueeze(1).to_broadcast([P, PACK, K]), op=ALU.add,
-            )
-
         def lowest_negated_logit(g):
-            lowest = work.tile([P, PACK], F32)
+            lowest = near.tile([P, PACK], F32)
             nc.vector.tensor_reduce(
                 out=lowest[:], in_=kept["neg_sl", g][:], axis=mybir.AxisListType.X, op=ALU.min
             )
             kept["lowest", g] = lowest
 
         def exponentials(g):
-            e = work.tile([P, PACK, K], F32)
-            e_sum = work.tile([P, PACK], F32)
+            e = near.tile([P, PACK, K], F32)
+            e_sum = near.tile([P, PACK], F32)
             for t in range(PACK):
                 nc.scalar.activation(
                     out=e[:, t, :], in_=kept["neg_sl", g][:, t, :], func=ACT.Exp,
@@ -206,12 +220,12 @@ def tile_depnet_pa_k_kernel(tc, xb, codewords, scale, out):
             kept["e_sum", g] = e_sum
 
         def invert_sums(g):
-            inv_sum = work.tile([P, PACK], F32)
+            inv_sum = near.tile([P, PACK], F32)
             nc.vector.reciprocal(out=inv_sum[:], in_=kept["e_sum", g][:])
             kept["inv_sum", g] = inv_sum
 
         def normalise(g):
-            a_grouped = work.tile([P, K * PACK], BF16, align_bytes=64)
+            a_grouped = near.tile([P, K * PACK], BF16, align_bytes=64)
             nc.vector.tensor_tensor(
                 out=a_grouped[:].rearrange("m (k t) -> m k t", t=PACK),
                 in0=kept["e", g][:].rearrange("m t k -> m k t"),
@@ -221,41 +235,44 @@ def tile_depnet_pa_k_kernel(tc, xb, codewords, scale, out):
             kept["a_grouped", g] = a_grouped
 
         def quantise_weights(g):
-            a_codes = work.tile([P, K], U32, align_bytes=64)
-            a_scales = work.tile([P, K], U8, align_bytes=64)
+            a_codes = near.tile([P, K], U32, align_bytes=64)
+            a_scales = near.tile([P, K], U8, align_bytes=64)
             quantise(nc, kept["a_grouped", g][:], a_codes[:], a_scales[:])
             kept["a_codes", g] = a_codes
             kept["a_scales", g] = a_scales
 
         def second_product(g):
             b = g // GROUPS_PER_IMAGE
-            first = g % GROUPS_PER_IMAGE == 0
-            last = g % GROUPS_PER_IMAGE == GROUPS_PER_IMAGE - 1
-            if first:
+            if g % GROUPS_PER_IMAGE == 0:
                 agg = ps_agg.tile([K, D], F32)
-                a_sum = ps_sum.tile([K, 1], F32)
                 kept["agg", b] = agg
-                kept["a_sum", b] = a_sum
             nc.tensor.matmul_mx(
                 out=kept["agg", b][:],
                 lhsT=kept["a_codes", g][:].bitcast(FP8X4),
                 lhsT_scale=kept["a_scales", g][:],
                 rhs=kept["xn_codes", g][:].bitcast(FP8X4),
                 rhs_scale=kept["xn_scales", g][:],
-                start=first,
-                stop=last,
+                start=g % GROUPS_PER_IMAGE == 0,
+                stop=g % GROUPS_PER_IMAGE == GROUPS_PER_IMAGE - 1,
             )
+
+        def sum_weights(g):
+            b = g // GROUPS_PER_IMAGE
+            if g % GROUPS_PER_IMAGE == 0:
+                a_sum = ps_sum.tile([K, 1], F32)
+                kept["a_sum", b] = a_sum
             for t in range(PACK):
                 nc.tensor.matmul(
                     out=kept["a_sum", b][:], lhsT=kept["e", g][:, t, :],
                     rhs=kept["inv_sum", g][:, t : t + 1],
-                    start=first and t == 0, stop=last and t == PACK - 1,
+                    start=g % GROUPS_PER_IMAGE == 0 and t == 0,
+                    stop=g % GROUPS_PER_IMAGE == GROUPS_PER_IMAGE - 1 and t == PACK - 1,
                 )
 
         def finish_image(b):
-            minus_a_sum = work.tile([K, 1], F32)
+            minus_a_sum = near.tile([K, 1], F32)
             nc.vector.tensor_scalar_mul(out=minus_a_sum[:], in0=kept["a_sum", b][:], scalar1=-1.0)
-            result = work.tile([K, D], F32)
+            result = near.tile([K, D], F32)
             nc.vector.scalar_tensor_tensor(
                 out=result[:].rearrange("k (q j) -> k q j", j=PACK),
                 in0=c_sb[:].rearrange("k (q j) -> k q j", j=PACK),
@@ -272,26 +289,29 @@ def tile_depnet_pa_k_kernel(tc, xb, codewords, scale, out):
         with tc.manual_schedule():
             for c in range(LOADS_AHEAD):
                 load(c)
-            for i in range(GROUPS + DEPTH):
+            for i in range(GROUPS + LAST_LAG + 1):
                 if i % GROUPS_PER_LOAD == 0 and i // GROUPS_PER_LOAD + LOADS_AHEAD < LOADS:
                     load(i // GROUPS_PER_LOAD + LOADS_AHEAD)
 
-                run(first_product, i - 1)
-                run(second_product, i - 5)
                 run(transpose_words, i)
+                run(transpose_logits, i - 3)
+                run(first_product, i - 1)
+                run(second_product, i - 7)
+                run(sum_weights, i - 7)
 
-                run(copy_words_out, i - 1)
-                run(exponentials, i - 3)
-                run(square_norms, i - 1)
+                run(codeword_factors, i - 2)
+                run(copy_first_half_out, i - 1)
+                run(exponentials, i - 5)
+                run(square_norms, i - 2)
 
-                if i >= 6 and (i - 6) % GROUPS_PER_IMAGE == GROUPS_PER_IMAGE - 1:
-                    finish_image((i - 6) // GROUPS_PER_IMAGE)
-                run(invert_sums, i - 4)
+                if i >= LAST_LAG and (i - LAST_LAG) % GROUPS_PER_IMAGE == GROUPS_PER_IMAGE - 1:
+                    finish_image((i - LAST_LAG) // GROUPS_PER_IMAGE)
+                run(add_position_term, i - 4)
+                run(invert_sums, i - 6)
                 run(regroup_channels, i)
-                run(scale_distances, i - 2)
-                run(normalise, i - 4)
-                run(add_codeword_term, i - 2)
+                run(lowest_negated_logit, i - 4)
+                run(normalise, i - 6)
                 run(quantise_along_channels, i)
-                run(lowest_negated_logit, i - 2)
-                run(quantise_weights, i - 4)
+                run(copy_second_half_out, i - 1)
+                run(quantise_weights, i - 6)
                 run(quantise_along_positions, i - 2)

@@ -23,7 +23,7 @@ GROUPS = B * GROUPS_PER_IMAGE
 LOADS_PER_IMAGE = N // LOAD
 LOADS = B * LOADS_PER_IMAGE
 LOADS_AHEAD = 2
-LAST_LAG = 8
+LAST_LAG = 9
 NEAR = 4
 FAR = 7
 
@@ -226,7 +226,7 @@ def tile_depnet_pa_k_kernel(tc, xb, codewords, scale, out):
 
         def normalise(g):
             a_grouped = near.tile([P, K * PACK], BF16, align_bytes=64)
-            nc.vector.tensor_tensor(
+            nc.gpsimd.tensor_tensor(
                 out=a_grouped[:].rearrange("m (k t) -> m k t", t=PACK),
                 in0=kept["e", g][:].rearrange("m t k -> m k t"),
                 in1=kept["inv_sum", g][:].unsqueeze(1).to_broadcast([P, K, PACK]),
@@ -296,7 +296,7 @@ def tile_depnet_pa_k_kernel(tc, xb, codewords, scale, out):
                 run(transpose_words, i)
                 run(transpose_logits, i - 3)
                 run(first_product, i - 1)
-                run(second_product, i - 7)
+                run(second_product, i - 8)
                 run(sum_weights, i - 7)
 
                 run(codeword_factors, i - 2)
@@ -306,12 +306,13 @@ def tile_depnet_pa_k_kernel(tc, xb, codewords, scale, out):
 
                 if i >= LAST_LAG and (i - LAST_LAG) % GROUPS_PER_IMAGE == GROUPS_PER_IMAGE - 1:
                     finish_image((i - LAST_LAG) // GROUPS_PER_IMAGE)
-                run(add_position_term, i - 4)
                 run(invert_sums, i - 6)
-                run(regroup_channels, i)
-                run(lowest_negated_logit, i - 4)
-                run(normalise, i - 6)
-                run(quantise_along_channels, i)
+                run(add_position_term, i - 4)
                 run(copy_second_half_out, i - 1)
-                run(quantise_weights, i - 6)
+                run(lowest_negated_logit, i - 4)
+                run(regroup_channels, i)
+                run(quantise_weights, i - 7)
                 run(quantise_along_positions, i - 2)
+                run(quantise_along_channels, i)
+
+                run(normalise, i - 6)

@@ -116,16 +116,15 @@ def tile_depnet_pa_k_kernel(tc, xb, codewords, scale, out):
             x_words = (
                 kept["x", g // GROUPS_PER_LOAD][:]
                 .bitcast(F32)
-                .rearrange("q (j m v) -> q j m v", j=PACK, v=2)
+                .rearrange("q (j g u m) -> q j g u m", j=PACK, u=2, m=P)
             )
-            first_m = (g % GROUPS_PER_LOAD) * P
             for half in range(2):
                 xt = ps_words.tile([P, 2, HALF], F32, tag="words")
                 for jj in range(2):
-                    for v in range(2):
+                    for u in range(2):
                         nc.tensor.transpose(
-                            xt[:, v, jj * P : (jj + 1) * P],
-                            x_words[:, 2 * half + jj, first_m : first_m + P, v],
+                            xt[:, u, jj * P : (jj + 1) * P],
+                            x_words[:, 2 * half + jj, g % GROUPS_PER_LOAD, u, :],
                             ident[:],
                         )
                 kept["xt", g, half] = xt
@@ -134,10 +133,10 @@ def tile_depnet_pa_k_kernel(tc, xb, codewords, scale, out):
             if half == 0:
                 xn_grouped = near.tile([P, D * PACK], BF16, align_bytes=64)
                 kept["xn_grouped", g] = xn_grouped
-            xn_words = kept["xn_grouped", g][:].bitcast(F32).rearrange("m (d v) -> m d v", v=2)
+            xn_words = kept["xn_grouped", g][:].bitcast(F32).rearrange("m (d u) -> m d u", u=2)
             copy(
                 out=xn_words[:, half * HALF : (half + 1) * HALF, :],
-                in_=kept["xt", g, half][:].rearrange("m v d -> m d v"),
+                in_=kept["xt", g, half][:].rearrange("m u d -> m d u"),
             )
 
         def copy_first_half_out(g):
@@ -180,7 +179,8 @@ def tile_depnet_pa_k_kernel(tc, xb, codewords, scale, out):
         def codeword_factors(g):
             y = near.tile([K, PACK, P], F32)
             nc.scalar.activation(
-                out=y[:], in_=kept["xc", g][:].rearrange("k (m t) -> k t m", t=PACK),
+                out=y[:].rearrange("k (u e) m -> k u e m", e=2),
+                in_=kept["xc", g][:].rearrange("k (u m e) -> k u e m", u=2, e=2),
                 func=ACT.Identity, scale=two_s[:, 0:1], bias=minus_s_c2[:, 0:1],
             )
             kept["y", g] = y

from contextlib import ExitStack

from concourse import mybir
from concourse.masks import make_identity

F32 = mybir.dt.float32
BF16 = mybir.dt.bfloat16
U32 = mybir.dt.uint32
U8 = mybir.dt.uint8
FP8X4 = mybir.dt.float8_e4m3fn_x4
ALU = mybir.AluOpType
ACT = mybir.ActivationFunctionType

P = 128
PACK = 4
B, D, N, K = 2, 512, 128 * 128, 128
GROUP = P * PACK
LOAD = 4 * GROUP
HALF = D // 2
GROUPS_PER_LOAD = LOAD // GROUP
GROUPS_PER_IMAGE = N // GROUP
GROUPS = B * GROUPS_PER_IMAGE
LOADS_PER_IMAGE = N // LOAD
LOADS = B * LOADS_PER_IMAGE
LOADS_AHEAD = 2
LAST_LAG = 9
NEAR = 4
FAR = 7

FLOPS = 2 * (2 * B * N * K * D)


def quantise(nc, values, codes, scales):
    nc.vector.quantize_mx(out=codes.bitcast(FP8X4), scales=scales, in_=values)


def tile_depnet_pa_k_kernel(tc, xb, codewords, scale, out):
    nc = tc.nc
    with ExitStack() as stack:
        consts = stack.enter_context(tc.tile_pool(name="consts", bufs=1))
        loads = stack.enter_context(tc.tile_pool(name="loads", bufs=LOADS_AHEAD + 1))
        near = stack.enter_context(tc.tile_pool(name="near", bufs=NEAR))
        far = stack.enter_context(tc.tile_pool(name="far", bufs=FAR))
        ps_words = stack.enter_context(tc.psum_pool(name="ps_words", bufs=4))
        ps_xc = stack.enter_context(tc.psum_pool(name="ps_xc", bufs=1))
        ps_y = stack.enter_context(tc.psum_pool(name="ps_y", bufs=1))
        ps_agg = stack.enter_context(tc.psum_pool(name="ps_agg", bufs=1))
        ps_sum = stack.enter_context(tc.psum_pool(name="ps_sum", bufs=1))

        ident = consts.tile([P, P], F32)
        make_identity(nc, ident[:])

        c_sb = consts.tile([K, D], BF16)
        nc.sync.dma_start(out=c_sb[:], in_=codewords)
        s_bf = consts.tile([P, K], BF16)
        nc.scalar.dma_start(out=s_bf[:], in_=scale.partition_broadcast(P))

        c_words = c_sb[:].bitcast(F32).rearrange("k (q v) -> k v q", v=2)
        ct = ps_words.tile([P, 2, HALF], F32, tag="words")
        for v in range(2):
            nc.tensor.transpose(ct[:, v, 0:K], c_words[:, v, :], ident[:])
        c_grouped = consts.tile([P, K * PACK], BF16, align_bytes=64)
        nc.vector.tensor_copy(
            out=c_grouped[:].bitcast(F32).rearrange("q (k v) -> q k v", v=2),
            in_=ct[:, :, 0:K].rearrange("q v k -> q k v"),
        )
        c_codes = consts.tile([P, K], U32, align_bytes=64)
        c_scales = consts.tile([P, K], U8, align_bytes=64)
        quantise(nc, c_grouped[:], c_codes[:], c_scales[:])

        c_squares = consts.tile([K, D], F32)
        c2 = consts.tile([K, 1], F32)
        nc.scalar.activation(out=c_squares[:], in_=c_sb[:], func=ACT.Square, accum_out=c2[:])

        minus_s = consts.tile([P, K], F32)
        nc.vector.tensor_scalar_mul(out=minus_s[:], in0=s_bf[:], scalar1=-1.0)
        minus_s_cols = ps_words.tile([P, 2, HALF], F32, tag="words")
        nc.tensor.transpose(minus_s_cols[:, 0, 0:P], minus_s[:], ident[:])
        two_s = consts.tile([K, 1], F32)
        nc.vector.tensor_scalar_mul(out=two_s[:], in0=minus_s_cols[:, 0, 0:1], scalar1=-2.0)
        minus_s_c2 = consts.tile([K, 1], F32)
        nc.vector.tensor_tensor(
            out=minus_s_c2[:], in0=minus_s_cols[:, 0, 0:1], in1=c2[:], op=ALU.mult
        )

        kept = {}

        def load(c):
            x_rows = xb[c // LOADS_PER_IMAGE].rearrange("(q j) h w -> q j (h w)", j=PACK)
            first_n = (c % LOADS_PER_IMAGE) * LOAD
            x_sb = loads.tile([P, PACK * LOAD], BF16)
            nc.sync.dma_start(
                out=x_sb[:].rearrange("q (j n) -> q j n", j=PACK),
                in_=x_rows[:, :, first_n : first_n + LOAD],
            )
            kept["x", c] = x_sb

        def regroup_channels(g):
            x_bf = kept["x", g // GROUPS_PER_LOAD][:].rearrange("q (j n) -> q j n", j=PACK)
            first_n = (g % GROUPS_PER_LOAD) * GROUP
            xd_grouped = near.tile([P, GROUP * PACK], BF16, align_bytes=64)
            nc.vector.tensor_copy(
                out=xd_grouped[:].rearrange("q (c i j) -> q c j i", i=4, j=PACK),
                in_=x_bf[:, :, first_n : first_n + GROUP].rearrange("q j (c i) -> q c j i", i=4),
            )
            kept["xd_grouped", g] = xd_grouped

        def quantise_along_channels(g):
            xd_codes = near.tile([P, GROUP], U32, align_bytes=64)
            xd_scales = near.tile([P, GROUP], U8, align_bytes=64)
            quantise(nc, kept["xd_grouped", g][:], xd_codes[:], xd_scales[:])
            kept["xd_codes", g] = xd_codes
            kept["xd_scales", g] = xd_scales

        def transpose_words(g):
            x_words = (
                kept["x", g // GROUPS_PER_LOAD][:]
                .bitcast(F32)
                .rearrange("q (j g u m) -> q j g u m", j=PACK, u=2, m=P)
            )
            for half in range(2):
                xt = ps_words.tile([P, 2, HALF], F32, tag="words")
                for jj in range(2):
                    for u in range(2):
                        nc.tensor.transpose(
                            xt[:, u, jj * P : (jj + 1) * P],
                            x_words[:, 2 * half + jj, g % GROUPS_PER_LOAD, u, :],
                            ident[:],
                        )
                kept["xt", g, half] = xt

        def copy_words_out(g, half, copy):
            if half == 0:
                xn_grouped = near.tile([P, D * PACK], BF16, align_bytes=64)
                kept["xn_grouped", g] = xn_grouped
            xn_words = kept["xn_grouped", g][:].bitcast(F32).rearrange("m (d u) -> m d u", u=2)
            copy(
                out=xn_words[:, half * HALF : (half + 1) * HALF, :],
                in_=kept["xt", g, half][:].rearrange("m u d -> m d u"),
            )

        def copy_first_half_out(g):
            copy_words_out(g, 0, nc.scalar.copy)

        def copy_second_half_out(g):
            copy_words_out(g, 1, nc.vector.tensor_copy)

        def quantise_along_positions(g):
            xn_codes = far.tile([P, D], U32, align_bytes=64)
            xn_scales = far.tile([P, D], U8, align_bytes=64)
            quantise(nc, kept["xn_grouped", g][:], xn_codes[:], xn_scales[:])
            kept["xn_codes", g] = xn_codes
            kept["xn_scales", g] = xn_scales

        def square_norms(g):
            x2 = far.tile([P, PACK], F32)
            xn_by_quarter = kept["xn_grouped", g][:].rearrange("m (d t) -> m t d", t=PACK)
            for t in range(PACK):
                squares = far.tile([P, D], BF16)
                nc.scalar.activation(
                    out=squares[:], in_=xn_by_quarter[:, t, :], func=ACT.Square,
                    accum_out=x2[:, t : t + 1],
                )
            kept["x2", g] = x2

        def first_product(g):
            xc = ps_xc.tile([K, GROUP], F32)
            nc.tensor.matmul_mx(
                out=xc[:],
                lhsT=c_codes[:].bitcast(FP8X4),
                lhsT_scale=c_scales[:],
                rhs=kept["xd_codes", g][:].bitcast(FP8X4),
                rhs_scale=kept["xd_scales", g][:],
                start=True,
                stop=True,
            )
            kept["xc", g] = xc

        def codeword_factors(g):
            y = near.tile([K, PACK, P], F32)
            nc.scalar.activation(
                out=y[:].rearrange("k (u e) m -> k u e m", e=2),
                in_=kept["xc", g][:].rearrange("k (u m e) -> k u e m", u=2, e=2),
                func=ACT.Identity, scale=two_s[:, 0:1], bias=minus_s_c2[:, 0:1],
            )
            kept["y", g] = y

        def transpose_logits(g):
            y_rows = ps_y.tile([P, PACK, K], F32)
            for t in range(PACK):
                nc.tensor.transpose(y_rows[:, t, :], kept["y", g][:, t, :], ident[:])
            kept["y_rows", g] = y_rows

        def add_position_term(g):
            neg_sl = near.tile([P, PACK, K], F32)
            for t in range(PACK):
                nc.vector.scalar_tensor_tensor(
                    out=neg_sl[:, t, :], in0=minus_s[:], scalar=kept["x2", g][:, t : t + 1],
                    in1=kept["y_rows", g][:, t, :], op0=ALU.mult, op1=ALU.add,
                )
            kept["neg_sl", g] = neg_sl

        def lowest_negated_logit(g):
            lowest = near.tile([P, PACK], F32)
            nc.vector.tensor_reduce(
                out=lowest[:], in_=kept["neg_sl", g][:], axis=mybir.AxisListType.X, op=ALU.min
            )
            kept["lowest", g] = lowest

        def exponentials(g):
            e = near.tile([P, PACK, K], F32)
            e_sum = near.tile([P, PACK], F32)
            for t in range(PACK):
                nc.scalar.activation(
                    out=e[:, t, :], in_=kept["neg_sl", g][:, t, :], func=ACT.Exp,
                    bias=kept["lowest", g][:, t : t + 1], scale=-1.0,
                    accum_out=e_sum[:, t : t + 1],
                )
            kept["e", g] = e
            kept["e_sum", g] = e_sum

        def invert_sums(g):
            inv_sum = near.tile([P, PACK], F32)
            nc.vector.reciprocal(out=inv_sum[:], in_=kept["e_sum", g][:])
            kept["inv_sum", g] = inv_sum

        def normalise(g):
            a_grouped = near.tile([P, K * PACK], BF16, align_bytes=64)
            nc.gpsimd.tensor_tensor(
                out=a_grouped[:].rearrange("m (k t) -> m k t", t=PACK),
                in0=kept["e", g][:].rearrange("m t k -> m k t"),
                in1=kept["inv_sum", g][:].unsqueeze(1).to_broadcast([P, K, PACK]),
                op=ALU.mult,
            )
            kept["a_grouped", g] = a_grouped

        def quantise_weights(g):
            a_codes = near.tile([P, K], U32, align_bytes=64)
            a_scales = near.tile([P, K], U8, align_bytes=64)
            quantise(nc, kept["a_grouped", g][:], a_codes[:], a_scales[:])
            kept["a_codes", g] = a_codes
            kept["a_scales", g] = a_scales

        def second_product(g):
            b = g // GROUPS_PER_IMAGE
            if g % GROUPS_PER_IMAGE == 0:
                agg = ps_agg.tile([K, D], F32)
                kept["agg", b] = agg
            nc.tensor.matmul_mx(
                out=kept["agg", b][:],
                lhsT=kept["a_codes", g][:].bitcast(FP8X4),
                lhsT_scale=kept["a_scales", g][:],
                rhs=kept["xn_codes", g][:].bitcast(FP8X4),
                rhs_scale=kept["xn_scales", g][:],
                start=g % GROUPS_PER_IMAGE == 0,
                stop=g % GROUPS_PER_IMAGE == GROUPS_PER_IMAGE - 1,
            )

        def sum_weights(g):
            b = g // GROUPS_PER_IMAGE
            if g % GROUPS_PER_IMAGE == 0:
                a_sum = ps_sum.tile([K, 1], F32)
                kept["a_sum", b] = a_sum
            for t in range(PACK):
                nc.tensor.matmul(
                    out=kept["a_sum", b][:], lhsT=kept["e", g][:, t, :],
                    rhs=kept["inv_sum", g][:, t : t + 1],
                    start=g % GROUPS_PER_IMAGE == 0 and t == 0,
                    stop=g % GROUPS_PER_IMAGE == GROUPS_PER_IMAGE - 1 and t == PACK - 1,
                )

        def finish_image(b):
            minus_a_sum = near.tile([K, 1], F32)
            nc.vector.tensor_scalar_mul(out=minus_a_sum[:], in0=kept["a_sum", b][:], scalar1=-1.0)
            result = near.tile([K, D], F32)
            nc.vector.scalar_tensor_tensor(
                out=result[:].rearrange("k (q j) -> k q j", j=PACK),
                in0=c_sb[:].rearrange("k (q j) -> k q j", j=PACK),
                scalar=minus_a_sum[:, 0:1],
                in1=kept["agg", b][:].rearrange("k (j q) -> k q j", j=PACK),
                op0=ALU.mult, op1=ALU.add,
            )
            nc.sync.dma_start(out=out[b], in_=result[:])

        def run(stage, g):
            if 0 <= g < GROUPS:
                stage(g)

        with tc.manual_schedule():
            for c in range(LOADS_AHEAD):
                load(c)
            for i in range(GROUPS + LAST_LAG + 1):
                if i % GROUPS_PER_LOAD == 0 and i // GROUPS_PER_LOAD + LOADS_AHEAD < LOADS:
                    load(i // GROUPS_PER_LOAD + LOADS_AHEAD)

                run(transpose_words, i)
                run(transpose_logits, i - 3)
                run(first_product, i - 1)
                run(second_product, i - 8)
                run(sum_weights, i - 7)

                run(codeword_factors, i - 2)
                run(copy_first_half_out, i - 1)
                run(exponentials, i - 5)
                run(square_norms, i - 2)

                if i >= LAST_LAG and (i - LAST_LAG) % GROUPS_PER_IMAGE == GROUPS_PER_IMAGE - 1:
                    finish_image((i - LAST_LAG) // GROUPS_PER_IMAGE)
                run(invert_sums, i - 6)
                run(add_position_term, i - 4)
                run(copy_second_half_out, i - 1)
                run(lowest_negated_logit, i - 4)
                run(regroup_channels, i)
                run(quantise_weights, i - 7)
                run(quantise_along_positions, i - 2)
                run(quantise_along_channels, i)

                run(normalise, i - 6)
